import numpy as np
import ml_dtypes

BF16 = ml_dtypes.bfloat16


def bf(x):
    return np.asarray(x, np.float32).astype(BF16)


def f32(x):
    return np.asarray(x, np.float32)


def f64(x):
    return np.asarray(x).astype(np.float64)


def striped(idx):
    return np.tile(idx.reshape(-1, 16).T, (8, 1))


F, C, S, N = 128, 128, 1024, 512


def setup_inputs():
    return {"x": bf(np.random.standard_normal((F, N))), "w": bf(2.0 * np.random.standard_normal((F, C)) / np.sqrt(F)), "b": f32(0.5 * np.random.standard_normal((C, 1))), "base": f32(0.1 * np.random.random((C, S))), "offs": striped(np.random.permutation(S)[:N])}


def reference(x, w, b, base, offs):
    idx = offs[:16].T.reshape(-1)
    e = np.exp(f64(w).T @ f64(x) + f64(b))
    r = 1.0 / e.sum(axis=0, keepdims=True)
    out = f64(base).copy()
    out[:, idx] = e * r
    return out

@@ -1,0 +1,44 @@
+import concourse.mybir as mybir
+
+FP32 = mybir.dt.float32
+BF16 = mybir.dt.bfloat16
+U16 = mybir.dt.uint16
+EXP = mybir.ActivationFunctionType.Exp
+MULT = mybir.AluOpType.mult
+
+F, C, S, N = 128, 128, 1024, 512
+FLOPS = 2 * F * C * N + 2 * C * N
+
+
+def tile_netfv_kernel(tc, x, w, b, base, offs, out):
+    nc = tc.nc
+    with tc.tile_pool(name="held", bufs=1) as held, tc.psum_pool(name="psum", bufs=1) as psum:
+        offsets = held.tile([C, N // 16], U16, name="offsets")
+        frames = held.tile([F, N], BF16, name="frames")
+        weights = held.tile([F, C], BF16, name="weights")
+        bias = held.tile([C, 1], FP32, name="bias")
+        window = held.tile([C, S], FP32, name="window")
+        nc.sync.dma_start(frames[:], x)
+        nc.scalar.dma_start(weights[:], w)
+        nc.sync.dma_start(offsets[:], offs)
+        nc.scalar.dma_start(bias[:], b)
+        nc.gpsimd.dma_start(window[:], base)
+
+        ones = held.tile([C, C], BF16, name="ones")
+        nc.vector.memset(ones[:], 1.0)
+
+        z = psum.tile([C, N], FP32, name="z")
+        nc.tensor.matmul(z[:], weights[:], frames[:], start=True, stop=True)
+
+        e_bf = held.tile([C, N], BF16, name="e_bf")
+        nc.scalar.activation(e_bf[:], z[:], EXP, bias=bias[:])
+        e = held.tile([C, N], FP32, name="e")
+        nc.scalar.activation(e[:], z[:], EXP, bias=bias[:])
+
+        total = psum.tile([C, N], FP32, name="total")
+        nc.tensor.matmul(total[:], ones[:], e_bf[:], start=True, stop=True)
+        r = held.tile([C, N], FP32, name="r")
+        nc.vector.reciprocal(r[:], total[:])
+
+        nc.vector.tensor_tensor(window[:].indirect(offsets[:]), e[:], r[:], MULT)
+        nc.sync.dma_start(out, window[:])

@@ -1,4 +1,5 @@
 import concourse.mybir as mybir
+from concourse.masks import make_identity
 
 FP32 = mybir.dt.float32
 BF16 = mybir.dt.bfloat16
@@ -7,6 +8,7 @@ EXP = mybir.ActivationFunctionType.Exp
 MULT = mybir.AluOpType.mult
 
 F, C, S, N = 128, 128, 1024, 512
+P = 128
 FLOPS = 2 * F * C * N + 2 * C * N
 
 
@@ -24,8 +26,10 @@ def tile_netfv_kernel(tc, x, w, b, base, offs, out):
         nc.scalar.dma_start(bias[:], b)
         nc.gpsimd.dma_start(window[:], base)
 
-        ones = held.tile([C, C], BF16, name="ones")
-        nc.vector.memset(ones[:], 1.0)
+        one_column = held.tile([C, 1], BF16, name="one_column")
+        nc.vector.memset(one_column[:], 1.0)
+        identity = held.tile([P, P], FP32, name="identity")
+        make_identity(nc, identity[:])
 
         z = psum.tile([C, N], FP32, name="z")
         nc.tensor.matmul(z[:], weights[:], frames[:], start=True, stop=True)
@@ -35,10 +39,21 @@ def tile_netfv_kernel(tc, x, w, b, base, offs, out):
         e = held.tile([C, N], FP32, name="e")
         nc.scalar.activation(e[:], z[:], EXP, bias=bias[:])
 
-        total = psum.tile([C, N], FP32, name="total")
-        nc.tensor.matmul(total[:], ones[:], e_bf[:], start=True, stop=True)
+        totals = psum.tile([P, N // P], FP32, name="totals")
+        for q in range(N // P):
+            nc.tensor.matmul(
+                totals[:, q : q + 1], e_bf[:, q * P : (q + 1) * P], one_column[:], start=True, stop=True
+            )
+        r_column = held.tile([P, N // P], FP32, name="r_column")
+        nc.vector.reciprocal(r_column[:], totals[:])
+
+        r_psum = psum.tile([C, N], FP32, name="r_psum")
+        for q in range(N // P):
+            nc.tensor.transpose(
+                r_psum[:, q * P : (q + 1) * P], r_column[:, q : q + 1].to_broadcast([P, C]), identity[:]
+            )
         r = held.tile([C, N], FP32, name="r")
-        nc.vector.reciprocal(r[:], total[:])
+        nc.scalar.copy(r[:], r_psum[:])
 
         nc.vector.tensor_tensor(window[:].indirect(offsets[:]), e[:], r[:], MULT)
         nc.sync.dma_start(out, window[:])

@@ -28,6 +28,11 @@ def tile_netfv_kernel(tc, x, w, b, base, offs, out):
 
         one_column = held.tile([C, 1], BF16, name="one_column")
         nc.vector.memset(one_column[:], 1.0)
+
+        table_warmer = held.tile([P, 1], FP32, name="table_warmer")
+        nc.vector.memset(table_warmer[:], 0.0)
+        nc.scalar.activation(table_warmer[:], table_warmer[:], EXP)
+
         identity = held.tile([P, P], FP32, name="identity")
         make_identity(nc, identity[:])
 

@@ -11,10 +11,17 @@ F, C, S, N = 128, 128, 1024, 512
 P = 128
 FLOPS = 2 * F * C * N + 2 * C * N
 
+PIECES = 2
+H = N // PIECES
+
 
 def tile_netfv_kernel(tc, x, w, b, base, offs, out):
     nc = tc.nc
-    with tc.tile_pool(name="held", bufs=1) as held, tc.psum_pool(name="psum", bufs=1) as psum:
+    with (
+        tc.tile_pool(name="held", bufs=1) as held,
+        tc.tile_pool(name="work", bufs=PIECES) as work,
+        tc.psum_pool(name="psum", bufs=PIECES) as psum,
+    ):
         offsets = held.tile([C, N // 16], U16, name="offsets")
         frames = held.tile([F, N], BF16, name="frames")
         weights = held.tile([F, C], BF16, name="weights")
@@ -24,41 +31,45 @@ def tile_netfv_kernel(tc, x, w, b, base, offs, out):
         nc.scalar.dma_start(weights[:], w)
         nc.sync.dma_start(offsets[:], offs)
         nc.scalar.dma_start(bias[:], b)
-        nc.gpsimd.dma_start(window[:], base)
+        nc.sync.dma_start(window[:], base)
 
         one_column = held.tile([C, 1], BF16, name="one_column")
         nc.vector.memset(one_column[:], 1.0)
+        identity = held.tile([P, P], FP32, name="identity")
+        make_identity(nc, identity[:])
 
         table_warmer = held.tile([P, 1], FP32, name="table_warmer")
         nc.vector.memset(table_warmer[:], 0.0)
         nc.scalar.activation(table_warmer[:], table_warmer[:], EXP)
 
-        identity = held.tile([P, P], FP32, name="identity")
-        make_identity(nc, identity[:])
+        z, e_bf, e, r = [], [], [], []
+        for h in range(PIECES):
+            z.append(psum.tile([C, H], FP32, name="z"))
+            nc.tensor.matmul(z[h][:], weights[:], frames[:, h * H : (h + 1) * H], start=True, stop=True)
+            e_bf.append(work.tile([C, H], BF16, name="e_bf"))
+            nc.scalar.activation(e_bf[h][:], z[h][:], EXP, bias=bias[:])
 
-        z = psum.tile([C, N], FP32, name="z")
-        nc.tensor.matmul(z[:], weights[:], frames[:], start=True, stop=True)
+        for h in range(PIECES):
+            totals = psum.tile([P, H // P], FP32, name="totals")
+            for q in range(H // P):
+                nc.tensor.matmul(
+                    totals[:, q : q + 1], e_bf[h][:, q * P : (q + 1) * P], one_column[:], start=True, stop=True
+                )
+            r_column = work.tile([P, H // P], FP32, name="r_column")
+            nc.vector.reciprocal(r_column[:], totals[:])
 
-        e_bf = held.tile([C, N], BF16, name="e_bf")
-        nc.scalar.activation(e_bf[:], z[:], EXP, bias=bias[:])
-        e = held.tile([C, N], FP32, name="e")
-        nc.scalar.activation(e[:], z[:], EXP, bias=bias[:])
+            r_psum = psum.tile([C, H], FP32, name="r_psum")
+            for q in range(H // P):
+                nc.tensor.transpose(
+                    r_psum[:, q * P : (q + 1) * P], r_column[:, q : q + 1].to_broadcast([P, C]), identity[:]
+                )
 
-        totals = psum.tile([P, N // P], FP32, name="totals")
-        for q in range(N // P):
-            nc.tensor.matmul(
-                totals[:, q : q + 1], e_bf[:, q * P : (q + 1) * P], one_column[:], start=True, stop=True
-            )
-        r_column = held.tile([P, N // P], FP32, name="r_column")
-        nc.vector.reciprocal(r_column[:], totals[:])
+            e.append(work.tile([C, H], FP32, name="e"))
+            nc.scalar.activation(e[h][:], z[h][:], EXP, bias=bias[:])
+            r.append(work.tile([C, H], FP32, name="r"))
+            nc.scalar.copy(r[h][:], r_psum[:])
 
-        r_psum = psum.tile([C, N], FP32, name="r_psum")
-        for q in range(N // P):
-            nc.tensor.transpose(
-                r_psum[:, q * P : (q + 1) * P], r_column[:, q : q + 1].to_broadcast([P, C]), identity[:]
-            )
-        r = held.tile([C, N], FP32, name="r")
-        nc.scalar.copy(r[:], r_psum[:])
-
-        nc.vector.tensor_tensor(window[:].indirect(offsets[:]), e[:], r[:], MULT)
+        for h in range(PIECES):
+            piece = offsets[:, h * (H // 16) : (h + 1) * (H // 16)]
+            nc.vector.tensor_tensor(window[:].indirect(piece), e[h][:], r[h][:], MULT)
         nc.sync.dma_start(out, window[:])

@@ -11,16 +11,16 @@ F, C, S, N = 128, 128, 1024, 512
 P = 128
 FLOPS = 2 * F * C * N + 2 * C * N
 
-PIECES = 2
-H = N // PIECES
+WIDTHS = (P, N - P)
+STARTS = (0, P)
+PIECES = len(WIDTHS)
 
 
 def tile_netfv_kernel(tc, x, w, b, base, offs, out):
     nc = tc.nc
     with (
         tc.tile_pool(name="held", bufs=1) as held,
-        tc.tile_pool(name="work", bufs=PIECES) as work,
-        tc.psum_pool(name="psum", bufs=PIECES) as psum,
+        tc.psum_pool(name="psum", bufs=1) as psum,
     ):
         offsets = held.tile([C, N // 16], U16, name="offsets")
         frames = held.tile([F, N], BF16, name="frames")
@@ -44,32 +44,35 @@ def tile_netfv_kernel(tc, x, w, b, base, offs, out):
 
         z, e_bf, e, r = [], [], [], []
         for h in range(PIECES):
-            z.append(psum.tile([C, H], FP32, name="z"))
-            nc.tensor.matmul(z[h][:], weights[:], frames[:, h * H : (h + 1) * H], start=True, stop=True)
-            e_bf.append(work.tile([C, H], BF16, name="e_bf"))
+            z.append(psum.tile([C, WIDTHS[h]], FP32, name="z%d" % h))
+            nc.tensor.matmul(
+                z[h][:], weights[:], frames[:, STARTS[h] : STARTS[h] + WIDTHS[h]], start=True, stop=True
+            )
+            e_bf.append(held.tile([C, WIDTHS[h]], BF16, name="e_bf%d" % h))
             nc.scalar.activation(e_bf[h][:], z[h][:], EXP, bias=bias[:])
 
         for h in range(PIECES):
-            totals = psum.tile([P, H // P], FP32, name="totals")
-            for q in range(H // P):
+            blocks = WIDTHS[h] // P
+            totals = psum.tile([P, blocks], FP32, name="totals%d" % h)
+            for q in range(blocks):
                 nc.tensor.matmul(
                     totals[:, q : q + 1], e_bf[h][:, q * P : (q + 1) * P], one_column[:], start=True, stop=True
                 )
-            r_column = work.tile([P, H // P], FP32, name="r_column")
+            r_column = held.tile([P, blocks], FP32, name="r_column%d" % h)
             nc.vector.reciprocal(r_column[:], totals[:])
 
-            r_psum = psum.tile([C, H], FP32, name="r_psum")
-            for q in range(H // P):
+            r_psum = psum.tile([C, WIDTHS[h]], FP32, name="r_psum%d" % h)
+            for q in range(blocks):
                 nc.tensor.transpose(
                     r_psum[:, q * P : (q + 1) * P], r_column[:, q : q + 1].to_broadcast([P, C]), identity[:]
                 )
 
-            e.append(work.tile([C, H], FP32, name="e"))
+            e.append(held.tile([C, WIDTHS[h]], FP32, name="e%d" % h))
             nc.scalar.activation(e[h][:], z[h][:], EXP, bias=bias[:])
-            r.append(work.tile([C, H], FP32, name="r"))
+            r.append(held.tile([C, WIDTHS[h]], FP32, name="r%d" % h))
             nc.scalar.copy(r[h][:], r_psum[:])
 
         for h in range(PIECES):
-            piece = offsets[:, h * (H // 16) : (h + 1) * (H // 16)]
+            piece = offsets[:, STARTS[h] // 16 : (STARTS[h] + WIDTHS[h]) // 16]
             nc.vector.tensor_tensor(window[:].indirect(piece), e[h][:], r[h][:], MULT)
         nc.sync.dma_start(out, window[:])

@@ -33,8 +33,8 @@ def tile_netfv_kernel(tc, x, w, b, base, offs, out):
         nc.scalar.dma_start(bias[:], b)
         nc.sync.dma_start(window[:], base)
 
-        one_column = held.tile([C, 1], BF16, name="one_column")
-        nc.vector.memset(one_column[:], 1.0)
+        ones = held.tile([C, P], BF16, name="ones")
+        nc.vector.memset(ones[:], 1.0)
         identity = held.tile([P, P], FP32, name="identity")
         make_identity(nc, identity[:])
 
@@ -42,7 +42,7 @@ def tile_netfv_kernel(tc, x, w, b, base, offs, out):
         nc.vector.memset(table_warmer[:], 0.0)
         nc.scalar.activation(table_warmer[:], table_warmer[:], EXP)
 
-        z, e_bf, e, r = [], [], [], []
+        z, e_bf, e = [], [], []
         for h in range(PIECES):
             z.append(psum.tile([C, WIDTHS[h]], FP32, name="z%d" % h))
             nc.tensor.matmul(
@@ -51,26 +51,32 @@ def tile_netfv_kernel(tc, x, w, b, base, offs, out):
             e_bf.append(held.tile([C, WIDTHS[h]], BF16, name="e_bf%d" % h))
             nc.scalar.activation(e_bf[h][:], z[h][:], EXP, bias=bias[:])
 
+        totals_0 = psum.tile([C, P], FP32, name="totals_0")
+        nc.tensor.matmul(totals_0[:], ones[:], e_bf[0][:], start=True, stop=True)
+        r_0 = held.tile([C, P], FP32, name="r_0")
+        nc.vector.reciprocal(r_0[:], totals_0[:])
+
+        blocks = WIDTHS[1] // P
+        totals_1 = psum.tile([P, blocks], FP32, name="totals_1")
+        for q in range(blocks):
+            nc.tensor.matmul(
+                totals_1[:, q : q + 1], e_bf[1][:, q * P : (q + 1) * P], ones[:, 0:1], start=True, stop=True
+            )
+        r_column = held.tile([P, blocks], FP32, name="r_column")
+        nc.vector.reciprocal(r_column[:], totals_1[:])
+
+        r_psum = []
+        for q in range(blocks):
+            r_psum.append(psum.tile([C, P], FP32, name="r_psum%d" % q))
+            nc.tensor.transpose(r_psum[q][:], r_column[:, q : q + 1].to_broadcast([P, C]), identity[:])
+
         for h in range(PIECES):
-            blocks = WIDTHS[h] // P
-            totals = psum.tile([P, blocks], FP32, name="totals%d" % h)
-            for q in range(blocks):
-                nc.tensor.matmul(
-                    totals[:, q : q + 1], e_bf[h][:, q * P : (q + 1) * P], one_column[:], start=True, stop=True
-                )
-            r_column = held.tile([P, blocks], FP32, name="r_column%d" % h)
-            nc.vector.reciprocal(r_column[:], totals[:])
-
-            r_psum = psum.tile([C, WIDTHS[h]], FP32, name="r_psum%d" % h)
-            for q in range(blocks):
-                nc.tensor.transpose(
-                    r_psum[:, q * P : (q + 1) * P], r_column[:, q : q + 1].to_broadcast([P, C]), identity[:]
-                )
-
             e.append(held.tile([C, WIDTHS[h]], FP32, name="e%d" % h))
             nc.scalar.activation(e[h][:], z[h][:], EXP, bias=bias[:])
-            r.append(held.tile([C, WIDTHS[h]], FP32, name="r%d" % h))
-            nc.scalar.copy(r[h][:], r_psum[:])
+        r_1 = held.tile([C, WIDTHS[1]], FP32, name="r_1")
+        for q in range(blocks):
+            nc.scalar.copy(r_1[:, q * P : (q + 1) * P], r_psum[q][:])
+        r = [r_0, r_1]
 
         for h in range(PIECES):
             piece = offsets[:, STARTS[h] // 16 : (STARTS[h] + WIDTHS[h]) // 16]

@@ -14,6 +14,7 @@ FLOPS = 2 * F * C * N + 2 * C * N
 WIDTHS = (P, N - P)
 STARTS = (0, P)
 PIECES = len(WIDTHS)
+FIRST_PARTS = 2
 
 
 def tile_netfv_kernel(tc, x, w, b, base, offs, out):
@@ -49,12 +50,19 @@ def tile_netfv_kernel(tc, x, w, b, base, offs, out):
                 z[h][:], weights[:], frames[:, STARTS[h] : STARTS[h] + WIDTHS[h]], start=True, stop=True
             )
             e_bf.append(held.tile([C, WIDTHS[h]], BF16, name="e_bf%d" % h))
-            nc.scalar.activation(e_bf[h][:], z[h][:], EXP, bias=bias[:])
+            parts = FIRST_PARTS if h == 0 else 1
+            part = WIDTHS[h] // parts
+            for k in range(parts):
+                columns = slice(k * part, (k + 1) * part)
+                nc.scalar.activation(e_bf[h][:, columns], z[h][:, columns], EXP, bias=bias[:])
 
-        totals_0 = psum.tile([C, P], FP32, name="totals_0")
-        nc.tensor.matmul(totals_0[:], ones[:], e_bf[0][:], start=True, stop=True)
         r_0 = held.tile([C, P], FP32, name="r_0")
-        nc.vector.reciprocal(r_0[:], totals_0[:])
+        part = P // FIRST_PARTS
+        for k in range(FIRST_PARTS):
+            columns = slice(k * part, (k + 1) * part)
+            totals_0 = psum.tile([C, part], FP32, name="totals_0_%d" % k)
+            nc.tensor.matmul(totals_0[:], ones[:], e_bf[0][:, columns], start=True, stop=True)
+            nc.vector.reciprocal(r_0[:, columns], totals_0[:])
 
         blocks = WIDTHS[1] // P
         totals_1 = psum.tile([P, blocks], FP32, name="totals_1")

@@ -14,7 +14,9 @@ FLOPS = 2 * F * C * N + 2 * C * N
 WIDTHS = (P, N - P)
 STARTS = (0, P)
 PIECES = len(WIDTHS)
-FIRST_PARTS = 2
+HALF = P // 2
+PART_WIDTHS = (HALF, HALF, N - P)
+PART_STARTS = (0, HALF, P)
 
 
 def tile_netfv_kernel(tc, x, w, b, base, offs, out):
@@ -28,8 +30,9 @@ def tile_netfv_kernel(tc, x, w, b, base, offs, out):
         weights = held.tile([F, C], BF16, name="weights")
         bias = held.tile([C, 1], FP32, name="bias")
         window = held.tile([C, S], FP32, name="window")
-        nc.sync.dma_start(frames[:], x)
+        nc.sync.dma_start(frames[:, 0 : N // 2], x[:, 0 : N // 2])
         nc.scalar.dma_start(weights[:], w)
+        nc.sync.dma_start(frames[:, N // 2 : N], x[:, N // 2 : N])
         nc.sync.dma_start(offsets[:], offs)
         nc.scalar.dma_start(bias[:], b)
         nc.sync.dma_start(window[:], base)
@@ -43,44 +46,39 @@ def tile_netfv_kernel(tc, x, w, b, base, offs, out):
         nc.vector.memset(table_warmer[:], 0.0)
         nc.scalar.activation(table_warmer[:], table_warmer[:], EXP)
 
-        z, e_bf, e = [], [], []
-        for h in range(PIECES):
-            z.append(psum.tile([C, WIDTHS[h]], FP32, name="z%d" % h))
-            nc.tensor.matmul(
-                z[h][:], weights[:], frames[:, STARTS[h] : STARTS[h] + WIDTHS[h]], start=True, stop=True
-            )
-            e_bf.append(held.tile([C, WIDTHS[h]], BF16, name="e_bf%d" % h))
-            parts = FIRST_PARTS if h == 0 else 1
-            part = WIDTHS[h] // parts
-            for k in range(parts):
-                columns = slice(k * part, (k + 1) * part)
-                nc.scalar.activation(e_bf[h][:, columns], z[h][:, columns], EXP, bias=bias[:])
+        z, e_bf = [], []
+        for k in range(len(PART_WIDTHS)):
+            z.append(psum.tile([C, PART_WIDTHS[k]], FP32, name="z%d" % k))
+            columns = slice(PART_STARTS[k], PART_STARTS[k] + PART_WIDTHS[k])
+            nc.tensor.matmul(z[k][:], weights[:], frames[:, columns], start=True, stop=True)
+            e_bf.append(held.tile([C, PART_WIDTHS[k]], BF16, name="e_bf%d" % k))
+            nc.scalar.activation(e_bf[k][:], z[k][:], EXP, bias=bias[:])
 
         r_0 = held.tile([C, P], FP32, name="r_0")
-        part = P // FIRST_PARTS
-        for k in range(FIRST_PARTS):
-            columns = slice(k * part, (k + 1) * part)
-            totals_0 = psum.tile([C, part], FP32, name="totals_0_%d" % k)
-            nc.tensor.matmul(totals_0[:], ones[:], e_bf[0][:, columns], start=True, stop=True)
-            nc.vector.reciprocal(r_0[:, columns], totals_0[:])
+        for k in range(2):
+            totals_0 = psum.tile([C, HALF], FP32, name="totals_0_%d" % k)
+            nc.tensor.matmul(totals_0[:], ones[:], e_bf[k][:], start=True, stop=True)
+            nc.vector.reciprocal(r_0[:, k * HALF : (k + 1) * HALF], totals_0[:])
 
         blocks = WIDTHS[1] // P
-        totals_1 = psum.tile([P, blocks], FP32, name="totals_1")
+        totals_1 = psum.tile([P, P], FP32, name="totals_1")
         for q in range(blocks):
             nc.tensor.matmul(
-                totals_1[:, q : q + 1], e_bf[1][:, q * P : (q + 1) * P], ones[:, 0:1], start=True, stop=True
+                totals_1[:, q : q + 1], e_bf[2][:, q * P : (q + 1) * P], ones[:, 0:1], start=True, stop=True
             )
         r_column = held.tile([P, blocks], FP32, name="r_column")
-        nc.vector.reciprocal(r_column[:], totals_1[:])
+        nc.vector.reciprocal(r_column[:], totals_1[:, 0:blocks])
 
         r_psum = []
         for q in range(blocks):
-            r_psum.append(psum.tile([C, P], FP32, name="r_psum%d" % q))
+            tag = "totals_1" if q == blocks - 1 else "r_psum%d" % q
+            r_psum.append(psum.tile([C, P], FP32, name="r_psum%d" % q, tag=tag))
             nc.tensor.transpose(r_psum[q][:], r_column[:, q : q + 1].to_broadcast([P, C]), identity[:])
 
-        for h in range(PIECES):
-            e.append(held.tile([C, WIDTHS[h]], FP32, name="e%d" % h))
-            nc.scalar.activation(e[h][:], z[h][:], EXP, bias=bias[:])
+        e = [held.tile([C, WIDTHS[h]], FP32, name="e%d" % h) for h in range(PIECES)]
+        for k in range(2):
+            nc.scalar.activation(e[0][:, k * HALF : (k + 1) * HALF], z[k][:], EXP, bias=bias[:])
+        nc.scalar.activation(e[1][:], z[2][:], EXP, bias=bias[:])
         r_1 = held.tile([C, WIDTHS[1]], FP32, name="r_1")
         for q in range(blocks):
             nc.scalar.copy(r_1[:, q * P : (q + 1) * P], r_psum[q][:])

import concourse.mybir as mybir
from concourse.masks import make_identity

FP32 = mybir.dt.float32
BF16 = mybir.dt.bfloat16
U16 = mybir.dt.uint16
EXP = mybir.ActivationFunctionType.Exp
MULT = mybir.AluOpType.mult

F, C, S, N = 128, 128, 1024, 512
P = 128
FLOPS = 2 * F * C * N + 2 * C * N

WIDTHS = (P, N - P)
STARTS = (0, P)
PIECES = len(WIDTHS)
HALF = P // 2
PART_WIDTHS = (HALF, HALF, N - P)
PART_STARTS = (0, HALF, P)


def tile_netfv_kernel(tc, x, w, b, base, offs, out):
    nc = tc.nc
    with (
        tc.tile_pool(name="held", bufs=1) as held,
        tc.psum_pool(name="psum", bufs=1) as psum,
    ):
        offsets = held.tile([C, N // 16], U16, name="offsets")
        frames = held.tile([F, N], BF16, name="frames")
        weights = held.tile([F, C], BF16, name="weights")
        bias = held.tile([C, 1], FP32, name="bias")
        window = held.tile([C, S], FP32, name="window")
        nc.sync.dma_start(frames[:, 0 : N // 2], x[:, 0 : N // 2])
        nc.scalar.dma_start(weights[:], w)
        nc.sync.dma_start(frames[:, N // 2 : N], x[:, N // 2 : N])
        nc.sync.dma_start(offsets[:], offs)
        nc.scalar.dma_start(bias[:], b)
        nc.sync.dma_start(window[:], base)

        ones = held.tile([C, P], BF16, name="ones")
        nc.vector.memset(ones[:], 1.0)
        identity = held.tile([P, P], FP32, name="identity")
        make_identity(nc, identity[:])

        table_warmer = held.tile([P, 1], FP32, name="table_warmer")
        nc.vector.memset(table_warmer[:], 0.0)
        nc.scalar.activation(table_warmer[:], table_warmer[:], EXP)

        z, e_bf = [], []
        for k in range(len(PART_WIDTHS)):
            z.append(psum.tile([C, PART_WIDTHS[k]], FP32, name="z%d" % k))
            columns = slice(PART_STARTS[k], PART_STARTS[k] + PART_WIDTHS[k])
            nc.tensor.matmul(z[k][:], weights[:], frames[:, columns], start=True, stop=True)
            e_bf.append(held.tile([C, PART_WIDTHS[k]], BF16, name="e_bf%d" % k))
            nc.scalar.activation(e_bf[k][:], z[k][:], EXP, bias=bias[:])

        r_0 = held.tile([C, P], FP32, name="r_0")
        for k in range(2):
            totals_0 = psum.tile([C, HALF], FP32, name="totals_0_%d" % k)
            nc.tensor.matmul(totals_0[:], ones[:], e_bf[k][:], start=True, stop=True)
            nc.vector.reciprocal(r_0[:, k * HALF : (k + 1) * HALF], totals_0[:])

        blocks = WIDTHS[1] // P
        totals_1 = psum.tile([P, P], FP32, name="totals_1")
        for q in range(blocks):
            nc.tensor.matmul(
                totals_1[:, q : q + 1], e_bf[2][:, q * P : (q + 1) * P], ones[:, 0:1], start=True, stop=True
            )
        r_column = held.tile([P, blocks], FP32, name="r_column")
        nc.vector.reciprocal(r_column[:], totals_1[:, 0:blocks])

        r_psum = []
        for q in range(blocks):
            tag = "totals_1" if q == blocks - 1 else "r_psum%d" % q
            r_psum.append(psum.tile([C, P], FP32, name="r_psum%d" % q, tag=tag))
            nc.tensor.transpose(r_psum[q][:], r_column[:, q : q + 1].to_broadcast([P, C]), identity[:])

        e = [held.tile([C, WIDTHS[h]], FP32, name="e%d" % h) for h in range(PIECES)]
        for k in range(2):
            nc.scalar.activation(e[0][:, k * HALF : (k + 1) * HALF], z[k][:], EXP, bias=bias[:])
        nc.scalar.activation(e[1][:], z[2][:], EXP, bias=bias[:])
        r_1 = held.tile([C, WIDTHS[1]], FP32, name="r_1")
        for q in range(blocks):
            nc.scalar.copy(r_1[:, q * P : (q + 1) * P], r_psum[q][:])
        r = [r_0, r_1]

        for h in range(PIECES):
            piece = offsets[:, STARTS[h] // 16 : (STARTS[h] + WIDTHS[h]) // 16]
            nc.vector.tensor_tensor(window[:].indirect(piece), e[h][:], r[h][:], MULT)
        nc.sync.dma_start(out, window[:])
